import numpy as np
import ml_dtypes


def mxq(x, axis, fmt="e4m3"):
    dtype, down = {"e4m3": (ml_dtypes.float8_e4m3fn, 7), "e5m2": (ml_dtypes.float8_e5m2, 14)}[fmt]
    v = np.moveaxis(np.asarray(x, np.float32).astype(ml_dtypes.bfloat16).astype(np.float64), axis, -1)
    blocks = v.reshape(v.shape[:-1] + (-1, 32))
    amax = np.abs(blocks).max(-1, keepdims=True)
    byte = np.maximum(np.where(amax > 0, np.frexp(amax)[1] - 1 + 127, 0) - down, 1)
    scale = np.exp2(byte - 127.0)
    codes = (blocks / scale).astype(np.float32).astype(dtype).astype(np.float64)
    return np.moveaxis((codes * scale).reshape(v.shape), -1, axis)


WIDE = False


def mx_kscale(k):
    if not WIDE:
        return np.ones(k)
    levels = np.array([10, -10, 5, -5, 0])
    a = np.random.permutation(np.resize(levels, k // 512 * 4)).reshape(k // 512, 4)
    idx = np.arange(k)
    return np.exp2(a[idx // 512, idx % 128 // 32])


BF16 = ml_dtypes.bfloat16


def bf(x):
    return np.asarray(x, np.float32).astype(BF16)


def f64(x):
    return np.asarray(x).astype(np.float64)


B, CI, CO, OH, OW, K = 4096, 32, 128, 2, 2, 4
STRIDE = 1
IH, IW = (OH - 1) * STRIDE + K, (OW - 1) * STRIDE + K
P = OH * OW
KC = CI * K * K


def extract_patches(x, out_h, out_w, k, stride):
    rows = []
    for di in range(k):
        cols = []
        for dj in range(k):
            cols.append(x[:, :, di:di + out_h * stride:stride, dj:dj + out_w * stride:stride])
        rows.append(np.stack(cols, axis=2))
    return np.stack(rows, axis=2)


def setup_inputs():
    s = mx_kscale(KC).reshape(CI, K * K)[:, 0]
    return {"in_spikes": bf(np.random.uniform(0.0, 1.0, (B, CI, IH, IW)) * s[None, :, None, None]),
            "weights": bf(np.random.standard_normal((OH, OW, CI, K, K, CO)) * 1.5 / np.sqrt(KC) / s[None, None, :, None, None, None])}


def reference(in_spikes, weights):
    out_h, out_w, _, k, _, _ = weights.shape
    patches = extract_patches(f64(in_spikes), out_h, out_w, k, STRIDE)
    p = patches.reshape(B, KC, P).transpose(2, 0, 1)
    w = f64(weights).reshape(P, KC, CO)
    out = mxq(p, 2, "e4m3") @ mxq(w, 1, "e4m3")
    return out.transpose(1, 2, 0).reshape(B, CO, OH, OW)

@@ -1,0 +1,184 @@
+from contextlib import ExitStack
+
+import concourse.mybir as mybir
+from concourse.masks import make_identity
+
+BF16 = mybir.dt.bfloat16
+F32 = mybir.dt.float32
+U32 = mybir.dt.uint32
+U8 = mybir.dt.uint8
+FP8X4 = mybir.dt.float8_e4m3fn_x4
+
+P = 128
+BATCH = 4096
+C_IN = 32
+C_OUT = 128
+IMG = 5
+WIN = 4
+OUT_HW = 2
+POSITIONS = OUT_HW * OUT_HW
+PIXELS = C_IN * IMG * IMG
+T = 2
+GROUPS = BATCH // (P * T)
+
+C_HI = 4
+C_LO = 8
+
+PAIR_COLUMNS = ((0, 1), (2, 1), (1, 3))
+PAIRS = len(PAIR_COLUMNS)
+ROW_WORDS = C_IN
+PLANE_WORDS = IMG * ROW_WORDS
+
+TILES = BATCH // P
+VECTOR_OUT_EVERY = 3
+
+FLOPS = 2 * BATCH * POSITIONS * C_IN * WIN * WIN * C_OUT
+
+
+def tile_stdpconvinhibit_t_kernel(tc, in_spikes, weights, out):
+    nc = tc.nc
+    x_view = in_spikes.rearrange("(n p t) c h w -> n p (t c h w)", p=P, t=T)
+    out_view = out.rearrange("(n p t) k i j -> n p (t k i j)", p=P, t=T)
+
+    with ExitStack() as stack:
+        keep = stack.enter_context(tc.tile_pool(name="keep", bufs=1))
+        x_pool = stack.enter_context(tc.tile_pool(name="x", bufs=GROUPS))
+        z_pool = stack.enter_context(tc.tile_pool(name="z", bufs=3))
+        grouped_pool = stack.enter_context(tc.tile_pool(name="grouped", bufs=3))
+        mx_pool = stack.enter_context(tc.tile_pool(name="mx", bufs=3))
+        o_pool = stack.enter_context(tc.tile_pool(name="o", bufs=3))
+        tr_pool = stack.enter_context(tc.psum_pool(name="tr", bufs=4))
+        acc_pool = stack.enter_context(tc.psum_pool(name="acc", bufs=3))
+        stack.enter_context(tc.manual_schedule())
+
+        x_tiles = []
+        w_raw = keep.tile([P, POSITIONS, WIN * C_OUT], BF16)
+        for n in range(GROUPS):
+            x_sb = x_pool.tile([P, T * PIXELS], BF16)
+            nc.sync.dma_start(out=x_sb[:], in_=x_view[n])
+            x_tiles.append(x_sb)
+            if n == 0:
+                for u in range(WIN):
+                    for g in range(C_HI):
+                        nc.sync.dma_start(
+                            out=w_raw[C_IN * u + g : C_IN * (u + 1) : C_HI, :, :],
+                            in_=weights[:, :, C_LO * g : C_LO * (g + 1), u, :, :].rearrange(
+                                "i j m v k -> m (i j) (v k)"
+                            ),
+                        )
+
+        identity = keep.tile([P, P], F32)
+        make_identity(nc, identity[:])
+
+        w_grouped = keep.tile([P, POSITIONS * C_OUT * WIN], BF16, align_bytes=64)
+        w_codes = keep.tile([P, POSITIONS * C_OUT], U32, align_bytes=64)
+        w_scales = keep.tile([P, POSITIONS * C_OUT], U8, align_bytes=64)
+
+        def quantise_weights():
+            w_raw_view = w_raw[:].rearrange("p (i j) (v k) -> p i j v k", j=OUT_HW, v=WIN)
+            w_grouped_view = w_grouped[:].rearrange("p (i j k t) -> p i j k t", i=OUT_HW, j=OUT_HW, t=WIN)
+            for j in range(OUT_HW):
+                for y in range(2):
+                    first, step = PAIR_COLUMNS[j + y]
+                    v0 = first - j
+                    nc.vector.tensor_copy(
+                        out=w_grouped_view[:, :, j, :, 2 * y : 2 * y + 2],
+                        in_=w_raw_view[:, :, j, v0 : v0 + step + 1 : step, :].rearrange("p i v k -> p i k v"),
+                    )
+            nc.vector.quantize_mx(out=w_codes[:].bitcast(FP8X4), scales=w_scales[:], in_=w_grouped[:])
+
+        z_tiles = {}
+        tr_tiles = {}
+        grouped_tiles = {}
+        mx_tiles = {}
+        acc_tiles = {}
+        o_tiles = {}
+
+        def make_pairs(q):
+            z = z_pool.tile([P, PAIRS * PLANE_WORDS * 2], BF16)
+            x_image = x_tiles[q // T][:, (q % T) * PIXELS : (q % T + 1) * PIXELS].rearrange(
+                "p (g m h w) -> p m h g w", g=C_HI, m=C_LO, h=IMG, w=IMG
+            )
+            for pair in range(PAIRS):
+                first, step = PAIR_COLUMNS[pair]
+                nc.vector.tensor_copy(
+                    out=z[:, pair * PLANE_WORDS * 2 : (pair + 1) * PLANE_WORDS * 2].rearrange(
+                        "p (h m g e) -> p m h g e", h=IMG, m=C_LO, g=C_HI, e=2
+                    ),
+                    in_=x_image[:, :, :, :, first : first + step + 1 : step],
+                )
+            z_tiles[q] = z
+
+        def transpose_pairs(q):
+            z_words = z_tiles.pop(q)[:].bitcast(F32)
+            for i in range(OUT_HW):
+                tr = tr_pool.tile([P, PAIRS, P], F32)
+                for pair in range(PAIRS):
+                    start = pair * PLANE_WORDS + i * ROW_WORDS
+                    nc.tensor.transpose(tr[:, pair, :], z_words[:, start : start + P], identity[:])
+                tr_tiles[(q, i)] = tr
+
+        def group_words(q):
+            grouped = grouped_pool.tile([P, POSITIONS * P * WIN], BF16, align_bytes=64)
+            grouped_words = grouped[:].bitcast(F32)
+            for i in range(OUT_HW):
+                tr = tr_tiles.pop((q, i))
+                for j in range(OUT_HW):
+                    s = i * OUT_HW + j
+                    nc.scalar.copy(
+                        out=grouped_words[:, s * P * 2 : (s + 1) * P * 2].rearrange("p (b y) -> p b y", y=2),
+                        in_=tr[:, j : j + 2, :].rearrange("p y b -> p b y"),
+                    )
+            grouped_tiles[q] = grouped
+
+        def quantise_patches(q):
+            codes = mx_pool.tile([P, POSITIONS * P], U32, align_bytes=64)
+            scales = mx_pool.tile([P, POSITIONS * P], U8, align_bytes=64)
+            nc.vector.quantize_mx(out=codes[:].bitcast(FP8X4), scales=scales[:], in_=grouped_tiles.pop(q)[:])
+            mx_tiles[q] = (codes, scales)
+
+        def multiply(q):
+            codes, scales = mx_tiles.pop(q)
+            acc = acc_pool.tile([P, POSITIONS, C_OUT], F32)
+            for s in range(POSITIONS):
+                nc.tensor.matmul_mx(
+                    out=acc[:, s, :],
+                    lhsT=codes[:, s * P : (s + 1) * P].bitcast(FP8X4),
+                    lhsT_scale=scales[:, s * P : (s + 1) * P],
+                    rhs=w_codes[:, s * C_OUT : (s + 1) * C_OUT].bitcast(FP8X4),
+                    rhs_scale=w_scales[:, s * C_OUT : (s + 1) * C_OUT],
+                    start=True,
+                    stop=True,
+                )
+            acc_tiles[q] = acc
+
+        def store(q):
+            n, t = divmod(q, T)
+            if t == 0:
+                o_new = o_pool.tile([P, T * C_OUT * POSITIONS], F32)
+                o_tiles[n] = o_new
+            o_sb = o_tiles[n]
+            o_part = o_sb[:, t * C_OUT * POSITIONS : (t + 1) * C_OUT * POSITIONS].rearrange(
+                "p (k s) -> p k s", s=POSITIONS
+            )
+            acc = acc_tiles.pop(q)
+            if q % VECTOR_OUT_EVERY == VECTOR_OUT_EVERY - 1:
+                nc.vector.tensor_copy(out=o_part, in_=acc[:].rearrange("p s k -> p k s"))
+            else:
+                nc.scalar.copy(out=o_part, in_=acc[:].rearrange("p s k -> p k s"))
+            if t == T - 1:
+                nc.sync.dma_start(out=out_view[n], in_=o_sb[:])
+
+        for step in range(TILES + 3):
+            if step < TILES:
+                make_pairs(step)
+                transpose_pairs(step)
+            if 0 <= step - 1 < TILES:
+                group_words(step - 1)
+            if step == 2:
+                quantise_weights()
+            if 0 <= step - 2 < TILES:
+                quantise_patches(step - 2)
+                multiply(step - 2)
+            if 0 <= step - 3:
+                store(step - 3)

@@ -30,7 +30,7 @@ ROW_WORDS = C_IN
 PLANE_WORDS = IMG * ROW_WORDS
 
 TILES = BATCH // P
-VECTOR_OUT_EVERY = 3
+VECTOR_OUT_EVERY = 2
 
 FLOPS = 2 * BATCH * POSITIONS * C_IN * WIN * WIN * C_OUT
 

@@ -30,7 +30,7 @@ ROW_WORDS = C_IN
 PLANE_WORDS = IMG * ROW_WORDS
 
 TILES = BATCH // P
-VECTOR_OUT_EVERY = 2
+VECTOR_OUT_EVERY = 3
 
 FLOPS = 2 * BATCH * POSITIONS * C_IN * WIN * WIN * C_OUT
 
@@ -140,13 +140,15 @@ def tile_stdpconvinhibit_t_kernel(tc, in_spikes, weights, out):
         def multiply(q):
             codes, scales = mx_tiles.pop(q)
             acc = acc_pool.tile([P, POSITIONS, C_OUT], F32)
+            acc_flat = acc[:].rearrange("p s k -> p (s k)")
             for s in range(POSITIONS):
+                columns = slice(s * C_OUT, min(s + 2, POSITIONS) * C_OUT)
                 nc.tensor.matmul_mx(
-                    out=acc[:, s, :],
+                    out=acc_flat[:, columns],
                     lhsT=codes[:, s * P : (s + 1) * P].bitcast(FP8X4),
                     lhsT_scale=scales[:, s * P : (s + 1) * P],
-                    rhs=w_codes[:, s * C_OUT : (s + 1) * C_OUT].bitcast(FP8X4),
-                    rhs_scale=w_scales[:, s * C_OUT : (s + 1) * C_OUT],
+                    rhs=w_codes[:, columns].bitcast(FP8X4),
+                    rhs_scale=w_scales[:, columns],
                     start=True,
                     stop=True,
                 )

@@ -5,6 +5,7 @@ from concourse.masks import make_identity
 
 BF16 = mybir.dt.bfloat16
 F32 = mybir.dt.float32
+I32 = mybir.dt.int32
 U32 = mybir.dt.uint32
 U8 = mybir.dt.uint8
 FP8X4 = mybir.dt.float8_e4m3fn_x4
@@ -18,7 +19,7 @@ WIN = 4
 OUT_HW = 2
 POSITIONS = OUT_HW * OUT_HW
 PIXELS = C_IN * IMG * IMG
-T = 2
+T = 4
 GROUPS = BATCH // (P * T)
 
 C_HI = 4
@@ -26,66 +27,97 @@ C_LO = 8
 
 PAIR_COLUMNS = ((0, 1), (2, 1), (1, 3))
 PAIRS = len(PAIR_COLUMNS)
-ROW_WORDS = C_IN
-PLANE_WORDS = IMG * ROW_WORDS
 
 TILES = BATCH // P
-VECTOR_OUT_EVERY = 3
+HALF = OUT_HW * P
+TOP, MID, LOW = range(3)
 
 FLOPS = 2 * BATCH * POSITIONS * C_IN * WIN * WIN * C_OUT
 
 
 def tile_stdpconvinhibit_t_kernel(tc, in_spikes, weights, out):
     nc = tc.nc
-    x_view = in_spikes.rearrange("(n p t) c h w -> n p (t c h w)", p=P, t=T)
-    out_view = out.rearrange("(n p t) k i j -> n p (t k i j)", p=P, t=T)
+    x_view = in_spikes.rearrange("(n p t) c h w -> n p t (c h w)", p=P, t=T)
+    out_view = out.rearrange("(n p t) k i j -> n p t (k i j)", p=P, t=T)
 
     with ExitStack() as stack:
         keep = stack.enter_context(tc.tile_pool(name="keep", bufs=1))
         x_pool = stack.enter_context(tc.tile_pool(name="x", bufs=GROUPS))
-        z_pool = stack.enter_context(tc.tile_pool(name="z", bufs=3))
-        grouped_pool = stack.enter_context(tc.tile_pool(name="grouped", bufs=3))
-        mx_pool = stack.enter_context(tc.tile_pool(name="mx", bufs=3))
+        z_pool = stack.enter_context(tc.tile_pool(name="z", bufs=4))
+        grouped_pool = stack.enter_context(tc.tile_pool(name="grouped", bufs=4))
+        mx_pool = stack.enter_context(tc.tile_pool(name="mx", bufs=4))
+        r_pool = stack.enter_context(tc.tile_pool(name="r", bufs=2))
         o_pool = stack.enter_context(tc.tile_pool(name="o", bufs=3))
         tr_pool = stack.enter_context(tc.psum_pool(name="tr", bufs=4))
-        acc_pool = stack.enter_context(tc.psum_pool(name="acc", bufs=3))
+        acc_pool = stack.enter_context(tc.psum_pool(name="acc", bufs=4))
         stack.enter_context(tc.manual_schedule())
 
-        x_tiles = []
         w_raw = keep.tile([P, POSITIONS, WIN * C_OUT], BF16)
+        x_tiles = []
         for n in range(GROUPS):
             x_sb = x_pool.tile([P, T * PIXELS], BF16)
-            nc.sync.dma_start(out=x_sb[:], in_=x_view[n])
             x_tiles.append(x_sb)
             if n == 0:
-                for u in range(WIN):
-                    for g in range(C_HI):
-                        nc.sync.dma_start(
-                            out=w_raw[C_IN * u + g : C_IN * (u + 1) : C_HI, :, :],
-                            in_=weights[:, :, C_LO * g : C_LO * (g + 1), u, :, :].rearrange(
-                                "i j m v k -> m (i j) (v k)"
-                            ),
-                        )
+                for t in range(T):
+                    nc.sync.dma_start(out=x_sb[:, t * PIXELS : (t + 1) * PIXELS], in_=x_view[n, :, t, :])
+                    if t == 1:
+                        nc.sync.dma_start(out=w_raw[:], in_=weights.rearrange("i j c u v k -> (c u) (i j) (v k)"))
+            else:
+                nc.sync.dma_start(out=x_sb[:].rearrange("p (t e) -> p t e", t=T), in_=x_view[n])
 
         identity = keep.tile([P, P], F32)
         make_identity(nc, identity[:])
 
-        w_grouped = keep.tile([P, POSITIONS * C_OUT * WIN], BF16, align_bytes=64)
-        w_codes = keep.tile([P, POSITIONS * C_OUT], U32, align_bytes=64)
-        w_scales = keep.tile([P, POSITIONS * C_OUT], U8, align_bytes=64)
+        place = keep.tile([P, 3, WIN, C_IN], BF16)
+        nc.gpsimd.memset(place[:, MID, 0, :], 0.0)
+        by_row = identity[:].rearrange("p (g m u) -> p u m g", g=C_HI, m=C_LO, u=WIN)
+        for part, group, u in (
+            [(TOP, u, u) for u in range(WIN)]
+            + [(MID, u + 1, u) for u in range(WIN - 1)]
+            + [(LOW, group, WIN - 1) for group in range(T)]
+        ):
+            nc.gpsimd.tensor_copy(
+                out=place[:, part, group, :].rearrange("p (m g) -> p m g", m=C_LO), in_=by_row[:, u, :, :]
+            )
 
-        def quantise_weights():
-            w_raw_view = w_raw[:].rearrange("p (i j) (v k) -> p i j v k", j=OUT_HW, v=WIN)
-            w_grouped_view = w_grouped[:].rearrange("p (i j k t) -> p i j k t", i=OUT_HW, j=OUT_HW, t=WIN)
+        w_codes = keep.tile([P, 3, HALF], U32, align_bytes=64)
+        w_scales = keep.tile([P, 3, HALF], U8, align_bytes=64)
+        w_low_codes = keep.tile([P, T, HALF], U32, align_bytes=64)
+        nc.gpsimd.memset(w_low_codes[:].bitcast(I32), 0)
+        w_grouped = keep.tile([P, 3, HALF * WIN], BF16, align_bytes=64)
+
+        def place_weights(part):
             for j in range(OUT_HW):
+                acc = acc_pool.tile([P, POSITIONS, C_OUT], F32)
+                nc.tensor.matmul(
+                    acc[:].rearrange("p s k -> p (s k)"),
+                    lhsT=place[:, part, :, :].rearrange("p u c -> p (u c)"),
+                    rhs=w_raw[:, (0 if part == TOP else OUT_HW) + j, :],
+                    start=True,
+                    stop=True,
+                )
+                grouped_view = w_grouped[:, part, j * P * WIN : (j + 1) * P * WIN].rearrange(
+                    "p (k t) -> p k t", t=WIN
+                )
                 for y in range(2):
                     first, step = PAIR_COLUMNS[j + y]
                     v0 = first - j
-                    nc.vector.tensor_copy(
-                        out=w_grouped_view[:, :, j, :, 2 * y : 2 * y + 2],
-                        in_=w_raw_view[:, :, j, v0 : v0 + step + 1 : step, :].rearrange("p i v k -> p i k v"),
+                    nc.scalar.copy(
+                        out=grouped_view[:, :, 2 * y : 2 * y + 2],
+                        in_=acc[:, v0 : v0 + step + 1 : step, :].rearrange("p v k -> p k v"),
                     )
-            nc.vector.quantize_mx(out=w_codes[:].bitcast(FP8X4), scales=w_scales[:], in_=w_grouped[:])
+
+        def quantise_weights(part):
+            nc.vector.quantize_mx(
+                out=w_codes[:, part, :].bitcast(FP8X4), scales=w_scales[:, part, :], in_=w_grouped[:, part, :]
+            )
+
+        def spread_low_weights():
+            for t in range(T):
+                rows = slice(t * C_IN, (t + 1) * C_IN)
+                nc.vector.tensor_copy(
+                    out=w_low_codes[rows, t, :].bitcast(I32), in_=w_codes[rows, LOW, :].bitcast(I32)
+                )
 
         z_tiles = {}
         tr_tiles = {}
@@ -95,92 +127,145 @@ def tile_stdpconvinhibit_t_kernel(tc, in_spikes, weights, out):
         o_tiles = {}
 
         def make_pairs(q):
-            z = z_pool.tile([P, PAIRS * PLANE_WORDS * 2], BF16)
+            z = z_pool.tile([P, PAIRS * P * 2], BF16)
             x_image = x_tiles[q // T][:, (q % T) * PIXELS : (q % T + 1) * PIXELS].rearrange(
                 "p (g m h w) -> p m h g w", g=C_HI, m=C_LO, h=IMG, w=IMG
             )
             for pair in range(PAIRS):
                 first, step = PAIR_COLUMNS[pair]
                 nc.vector.tensor_copy(
-                    out=z[:, pair * PLANE_WORDS * 2 : (pair + 1) * PLANE_WORDS * 2].rearrange(
-                        "p (h m g e) -> p m h g e", h=IMG, m=C_LO, g=C_HI, e=2
+                    out=z[:, pair * P * 2 : (pair + 1) * P * 2].rearrange(
+                        "p (h m g e) -> p m h g e", h=WIN, m=C_LO, g=C_HI, e=2
                     ),
-                    in_=x_image[:, :, :, :, first : first + step + 1 : step],
+                    in_=x_image[:, :, 0:WIN, :, first : first + step + 1 : step],
                 )
             z_tiles[q] = z
 
-        def transpose_pairs(q):
-            z_words = z_tiles.pop(q)[:].bitcast(F32)
-            for i in range(OUT_HW):
-                tr = tr_pool.tile([P, PAIRS, P], F32)
-                for pair in range(PAIRS):
-                    start = pair * PLANE_WORDS + i * ROW_WORDS
-                    nc.tensor.transpose(tr[:, pair, :], z_words[:, start : start + P], identity[:])
-                tr_tiles[(q, i)] = tr
+        def make_low_pairs(n):
+            z = z_pool.tile([P, PAIRS * P * 2], BF16)
+            x_image = x_tiles[n][:].rearrange(
+                "p (t g m h w) -> p m t h g w", t=T, g=C_HI, m=C_LO, h=IMG, w=IMG
+            )
+            for pair in range(PAIRS):
+                first, step = PAIR_COLUMNS[pair]
+                nc.vector.tensor_copy(
+                    out=z[:, pair * P * 2 : (pair + 1) * P * 2].rearrange(
+                        "p (t m g e) -> p m t g e", t=T, m=C_LO, g=C_HI, e=2
+                    ),
+                    in_=x_image[:, :, :, IMG - 1, :, first : first + step + 1 : step],
+                )
+            z_tiles[("low", n)] = z
 
-        def group_words(q):
-            grouped = grouped_pool.tile([P, POSITIONS * P * WIN], BF16, align_bytes=64)
-            grouped_words = grouped[:].bitcast(F32)
-            for i in range(OUT_HW):
-                tr = tr_tiles.pop((q, i))
-                for j in range(OUT_HW):
-                    s = i * OUT_HW + j
-                    nc.scalar.copy(
-                        out=grouped_words[:, s * P * 2 : (s + 1) * P * 2].rearrange("p (b y) -> p b y", y=2),
-                        in_=tr[:, j : j + 2, :].rearrange("p y b -> p b y"),
-                    )
-            grouped_tiles[q] = grouped
+        def transpose_pairs(key):
+            z_words = z_tiles.pop(key)[:].bitcast(F32)
+            tr = tr_pool.tile([P, PAIRS, P], F32)
+            for pair in range(PAIRS):
+                nc.tensor.transpose(tr[:, pair, :], z_words[:, pair * P : (pair + 1) * P], identity[:])
+            tr_tiles[key] = tr
+
+        def group_words(key):
+            grouped = grouped_pool.tile([P, HALF * WIN], BF16, align_bytes=64)
+            grouped_words = grouped[:].bitcast(F32).rearrange("p (j b y) -> p j b y", j=OUT_HW, y=2)
+            tr = tr_tiles.pop(key)
+            for j in range(OUT_HW):
+                nc.scalar.copy(
+                    out=grouped_words[:, j, :, :], in_=tr[:, j : j + 2, :].rearrange("p y b -> p b y")
+                )
+            grouped_tiles[key] = grouped
 
         def quantise_patches(q):
-            codes = mx_pool.tile([P, POSITIONS * P], U32, align_bytes=64)
-            scales = mx_pool.tile([P, POSITIONS * P], U8, align_bytes=64)
-            nc.vector.quantize_mx(out=codes[:].bitcast(FP8X4), scales=scales[:], in_=grouped_tiles.pop(q)[:])
+            codes = mx_pool.tile([P, OUT_HW, HALF], U32, align_bytes=64)
+            scales = mx_pool.tile([P, OUT_HW, HALF], U8, align_bytes=64)
+            grouped = grouped_tiles.pop(q)
+            for i in range(OUT_HW):
+                nc.vector.quantize_mx(
+                    out=codes[:, i, :].bitcast(FP8X4), scales=scales[:, i, :], in_=grouped[:]
+                )
             mx_tiles[q] = (codes, scales)
 
+        def quantise_low(n):
+            codes = r_pool.tile([P, HALF], U32, align_bytes=64)
+            scales = r_pool.tile([P, HALF], U8, align_bytes=64)
+            nc.vector.quantize_mx(
+                out=codes[:].bitcast(FP8X4), scales=scales[:], in_=grouped_tiles.pop(("low", n))[:]
+            )
+            mx_tiles[("low", n)] = (codes, scales)
+
         def multiply(q):
+            n, t = divmod(q, T)
             codes, scales = mx_tiles.pop(q)
+            low_codes, low_scales = mx_tiles[("low", n)]
             acc = acc_pool.tile([P, POSITIONS, C_OUT], F32)
-            acc_flat = acc[:].rearrange("p s k -> p (s k)")
-            for s in range(POSITIONS):
-                columns = slice(s * C_OUT, min(s + 2, POSITIONS) * C_OUT)
+            for j in range(OUT_HW):
+                half = slice(j * P, (j + 1) * P)
                 nc.tensor.matmul_mx(
-                    out=acc_flat[:, columns],
-                    lhsT=codes[:, s * P : (s + 1) * P].bitcast(FP8X4),
-                    lhsT_scale=scales[:, s * P : (s + 1) * P],
-                    rhs=w_codes[:, columns].bitcast(FP8X4),
-                    rhs_scale=w_scales[:, columns],
+                    out=acc[:, j, :],
+                    lhsT=codes[:, 0, half].bitcast(FP8X4),
+                    lhsT_scale=scales[:, 0, half],
+                    rhs=w_codes[:, 0, half].bitcast(FP8X4),
+                    rhs_scale=w_scales[:, 0, half],
                     start=True,
+                    stop=True,
+                )
+            for j in range(OUT_HW):
+                half = slice(j * P, (j + 1) * P)
+                nc.tensor.matmul_mx(
+                    out=acc[:, OUT_HW + j, :],
+                    lhsT=codes[:, 1, half].bitcast(FP8X4),
+                    lhsT_scale=scales[:, 1, half],
+                    rhs=w_codes[:, 1, half].bitcast(FP8X4),
+                    rhs_scale=w_scales[:, 1, half],
+                    start=True,
+                    stop=False,
+                )
+                nc.tensor.matmul_mx(
+                    out=acc[:, OUT_HW + j, :],
+                    lhsT=low_codes[:, half].bitcast(FP8X4),
+                    lhsT_scale=low_scales[:, half],
+                    rhs=w_low_codes[:, t, half].bitcast(FP8X4),
+                    rhs_scale=w_scales[:, 2, half],
+                    start=False,
                     stop=True,
                 )
             acc_tiles[q] = acc
 
         def store(q):
             n, t = divmod(q, T)
-            if t == 0:
-                o_new = o_pool.tile([P, T * C_OUT * POSITIONS], F32)
-                o_tiles[n] = o_new
-            o_sb = o_tiles[n]
-            o_part = o_sb[:, t * C_OUT * POSITIONS : (t + 1) * C_OUT * POSITIONS].rearrange(
-                "p (k s) -> p k s", s=POSITIONS
+            o_sb = o_pool.tile([P, C_OUT * POSITIONS], F32)
+            nc.scalar.copy(
+                out=o_sb[:].rearrange("p (k s) -> p k s", s=POSITIONS),
+                in_=acc_tiles.pop(q)[:].rearrange("p s k -> p k s"),
             )
-            acc = acc_tiles.pop(q)
-            if q % VECTOR_OUT_EVERY == VECTOR_OUT_EVERY - 1:
-                nc.vector.tensor_copy(out=o_part, in_=acc[:].rearrange("p s k -> p k s"))
-            else:
-                nc.scalar.copy(out=o_part, in_=acc[:].rearrange("p s k -> p k s"))
-            if t == T - 1:
-                nc.sync.dma_start(out=out_view[n], in_=o_sb[:])
+            nc.sync.dma_start(out=out_view[n, :, t, :], in_=o_sb[:])
 
-        for step in range(TILES + 3):
+        for step in range(TILES + 4):
+            group, t = divmod(step, T)
             if step < TILES:
                 make_pairs(step)
                 transpose_pairs(step)
+                if step == 2 or (group > 0 and t == 0):
+                    make_low_pairs(group)
+                    transpose_pairs(("low", group))
+            if step == 0:
+                place_weights(TOP)
+            if step == 1:
+                place_weights(MID)
             if 0 <= step - 1 < TILES:
                 group_words(step - 1)
+                if step == 3 or (0 < group < GROUPS and t == 1):
+                    group_words(("low", group))
             if step == 2:
-                quantise_weights()
+                place_weights(LOW)
+                quantise_weights(TOP)
+                quantise_weights(MID)
             if 0 <= step - 2 < TILES:
                 quantise_patches(step - 2)
-                multiply(step - 2)
-            if 0 <= step - 3:
-                store(step - 3)
+                if step == 3:
+                    quantise_weights(LOW)
+                    spread_low_weights()
+                if step == 3 or (0 < group < GROUPS and t == 2):
+                    quantise_low(group)
+            if 0 <= step - 3 < TILES:
+                multiply(step - 3)
+            if 0 <= step - 4:
+                store(step - 4)

@@ -47,7 +47,7 @@ def tile_stdpconvinhibit_t_kernel(tc, in_spikes, weights, out):
         grouped_pool = stack.enter_context(tc.tile_pool(name="grouped", bufs=4))
         mx_pool = stack.enter_context(tc.tile_pool(name="mx", bufs=4))
         r_pool = stack.enter_context(tc.tile_pool(name="r", bufs=2))
-        o_pool = stack.enter_context(tc.tile_pool(name="o", bufs=3))
+        o_pool = stack.enter_context(tc.tile_pool(name="o", bufs=12))
         tr_pool = stack.enter_context(tc.psum_pool(name="tr", bufs=4))
         acc_pool = stack.enter_context(tc.psum_pool(name="acc", bufs=4))
         stack.enter_context(tc.manual_schedule())

@@ -25,10 +25,9 @@ GROUPS = BATCH // (P * T)
 C_HI = 4
 C_LO = 8
 
-PAIR_COLUMNS = ((0, 1), (2, 1), (1, 3))
-PAIRS = len(PAIR_COLUMNS)
-
 TILES = BATCH // P
+DUO = 2
+DUOS = TILES // DUO
 HALF = OUT_HW * P
 TOP, MID, LOW = range(3)
 
@@ -43,27 +42,29 @@ def tile_stdpconvinhibit_t_kernel(tc, in_spikes, weights, out):
     with ExitStack() as stack:
         keep = stack.enter_context(tc.tile_pool(name="keep", bufs=1))
         x_pool = stack.enter_context(tc.tile_pool(name="x", bufs=GROUPS))
-        z_pool = stack.enter_context(tc.tile_pool(name="z", bufs=4))
-        grouped_pool = stack.enter_context(tc.tile_pool(name="grouped", bufs=4))
-        mx_pool = stack.enter_context(tc.tile_pool(name="mx", bufs=4))
-        r_pool = stack.enter_context(tc.tile_pool(name="r", bufs=2))
+        z_pool = stack.enter_context(tc.tile_pool(name="z", bufs=6))
+        grouped_pool = stack.enter_context(tc.tile_pool(name="grouped", bufs=3))
+        low_pool = stack.enter_context(tc.tile_pool(name="low", bufs=3))
+        mx_pool = stack.enter_context(tc.tile_pool(name="mx", bufs=3))
         o_pool = stack.enter_context(tc.tile_pool(name="o", bufs=12))
         tr_pool = stack.enter_context(tc.psum_pool(name="tr", bufs=4))
         acc_pool = stack.enter_context(tc.psum_pool(name="acc", bufs=4))
         stack.enter_context(tc.manual_schedule())
 
         w_raw = keep.tile([P, POSITIONS, WIN * C_OUT], BF16)
+        w_view = weights.rearrange("i j c u v k -> (c u) (i j) (v k)")
         x_tiles = []
         for n in range(GROUPS):
-            x_sb = x_pool.tile([P, T * PIXELS], BF16)
+            x_sb = x_pool.tile([P, T, PIXELS], BF16)
             x_tiles.append(x_sb)
             if n == 0:
-                for t in range(T):
-                    nc.sync.dma_start(out=x_sb[:, t * PIXELS : (t + 1) * PIXELS], in_=x_view[n, :, t, :])
-                    if t == 1:
-                        nc.sync.dma_start(out=w_raw[:], in_=weights.rearrange("i j c u v k -> (c u) (i j) (v k)"))
+                nc.sync.dma_start(out=x_sb[:, 0:1, :], in_=x_view[n, :, 0:1, :])
+                nc.sync.dma_start(out=x_sb[:, 1:2, :], in_=x_view[n, :, 1:2, :])
+                nc.sync.dma_start(out=w_raw[:, 0:OUT_HW, :], in_=w_view[:, 0:OUT_HW, :])
+                nc.sync.dma_start(out=x_sb[:, 2:4, :], in_=x_view[n, :, 2:4, :])
+                nc.sync.dma_start(out=w_raw[:, OUT_HW:POSITIONS, :], in_=w_view[:, OUT_HW:POSITIONS, :])
             else:
-                nc.sync.dma_start(out=x_sb[:].rearrange("p (t e) -> p t e", t=T), in_=x_view[n])
+                nc.sync.dma_start(out=x_sb[:], in_=x_view[n])
 
         identity = keep.tile([P, P], F32)
         make_identity(nc, identity[:])
@@ -86,26 +87,23 @@ def tile_stdpconvinhibit_t_kernel(tc, in_spikes, weights, out):
         nc.gpsimd.memset(w_low_codes[:].bitcast(I32), 0)
         w_grouped = keep.tile([P, 3, HALF * WIN], BF16, align_bytes=64)
 
-        def place_weights(part):
-            for j in range(OUT_HW):
-                acc = acc_pool.tile([P, POSITIONS, C_OUT], F32)
+        def place_weights(part, copy):
+            acc = acc_pool.tile([P, OUT_HW, C_OUT * WIN], BF16)
+            for j, columns, words in (
+                (0, slice(0, 4, 1), slice(0, 4)),
+                (1, slice(1, 3, 1), slice(0, 2)),
+                (1, slice(0, 4, 3), slice(2, 4)),
+            ):
                 nc.tensor.matmul(
-                    acc[:].rearrange("p s k -> p (s k)"),
+                    acc[:, j, :].rearrange("p (k t) -> p t k", t=WIN)[:, words, :],
                     lhsT=place[:, part, :, :].rearrange("p u c -> p (u c)"),
-                    rhs=w_raw[:, (0 if part == TOP else OUT_HW) + j, :],
+                    rhs=w_raw[:, (0 if part == TOP else OUT_HW) + j, :].rearrange("p (v k) -> p v k", v=WIN)[
+                        :, columns, :
+                    ],
                     start=True,
                     stop=True,
                 )
-                grouped_view = w_grouped[:, part, j * P * WIN : (j + 1) * P * WIN].rearrange(
-                    "p (k t) -> p k t", t=WIN
-                )
-                for y in range(2):
-                    first, step = PAIR_COLUMNS[j + y]
-                    v0 = first - j
-                    nc.scalar.copy(
-                        out=grouped_view[:, :, 2 * y : 2 * y + 2],
-                        in_=acc[:, v0 : v0 + step + 1 : step, :].rearrange("p v k -> p k v"),
-                    )
+            copy(out=w_grouped[:, part, :], in_=acc[:].rearrange("p j e -> p (j e)"))
 
         def quantise_weights(part):
             nc.vector.quantize_mx(
@@ -120,152 +118,162 @@ def tile_stdpconvinhibit_t_kernel(tc, in_spikes, weights, out):
                 )
 
         z_tiles = {}
+        low_z = {}
         tr_tiles = {}
+        low_tr = {}
         grouped_tiles = {}
+        low_grouped = {}
         mx_tiles = {}
+        low_mx = {}
         acc_tiles = {}
-        o_tiles = {}
+
+        def new_z():
+            quads = z_pool.tile([P, P * 4], BF16)
+            pairs = z_pool.tile([P, P * 2], BF16)
+            return quads, pairs
 
         def make_pairs(q):
-            z = z_pool.tile([P, PAIRS * P * 2], BF16)
-            x_image = x_tiles[q // T][:, (q % T) * PIXELS : (q % T + 1) * PIXELS].rearrange(
+            quads, pairs = new_z()
+            image = x_tiles[q // T][:, q % T, :].rearrange(
                 "p (g m h w) -> p m h g w", g=C_HI, m=C_LO, h=IMG, w=IMG
-            )
-            for pair in range(PAIRS):
-                first, step = PAIR_COLUMNS[pair]
+            )[:, :, 0:WIN, :, :]
+            for z, width, columns in ((quads, 4, slice(0, 4, 1)), (pairs, 2, slice(1, 5, 3))):
                 nc.vector.tensor_copy(
-                    out=z[:, pair * P * 2 : (pair + 1) * P * 2].rearrange(
-                        "p (h m g e) -> p m h g e", h=WIN, m=C_LO, g=C_HI, e=2
-                    ),
-                    in_=x_image[:, :, 0:WIN, :, first : first + step + 1 : step],
+                    out=z[:].rearrange("p (h m g e) -> p m h g e", h=WIN, m=C_LO, g=C_HI, e=width),
+                    in_=image[:, :, :, :, columns],
                 )
-            z_tiles[q] = z
+            z_tiles[q] = (quads, pairs)
 
         def make_low_pairs(n):
-            z = z_pool.tile([P, PAIRS * P * 2], BF16)
-            x_image = x_tiles[n][:].rearrange(
-                "p (t g m h w) -> p m t h g w", t=T, g=C_HI, m=C_LO, h=IMG, w=IMG
-            )
-            for pair in range(PAIRS):
-                first, step = PAIR_COLUMNS[pair]
+            quads, pairs = new_z()
+            image = x_tiles[n][:].rearrange(
+                "p t (g m h w) -> p m t h g w", g=C_HI, m=C_LO, h=IMG, w=IMG
+            )[:, :, :, IMG - 1, :, :]
+            for z, width, columns in ((quads, 4, slice(0, 4, 1)), (pairs, 2, slice(1, 5, 3))):
                 nc.vector.tensor_copy(
-                    out=z[:, pair * P * 2 : (pair + 1) * P * 2].rearrange(
-                        "p (t m g e) -> p m t g e", t=T, m=C_LO, g=C_HI, e=2
-                    ),
-                    in_=x_image[:, :, :, IMG - 1, :, first : first + step + 1 : step],
+                    out=z[:].rearrange("p (t m g e) -> p m t g e", t=T, m=C_LO, g=C_HI, e=width),
+                    in_=image[:, :, :, :, columns],
                 )
-            z_tiles[("low", n)] = z
+            low_z[n] = (quads, pairs)
 
-        def transpose_pairs(key):
-            z_words = z_tiles.pop(key)[:].bitcast(F32)
-            tr = tr_pool.tile([P, PAIRS, P], F32)
-            for pair in range(PAIRS):
-                nc.tensor.transpose(tr[:, pair, :], z_words[:, pair * P : (pair + 1) * P], identity[:])
-            tr_tiles[key] = tr
+        def transpose_words(z):
+            quads, pairs = (part[:].bitcast(F32) for part in z)
+            tr = tr_pool.tile([P, 3, P], F32)
+            for plane, words in enumerate((quads[:, 0 : 2 * P : 2], quads[:, 1 : 2 * P : 2], pairs)):
+                nc.tensor.transpose(tr[:, plane, :], words, identity[:])
+            return tr
 
-        def group_words(key):
-            grouped = grouped_pool.tile([P, HALF * WIN], BF16, align_bytes=64)
-            grouped_words = grouped[:].bitcast(F32).rearrange("p (j b y) -> p j b y", j=OUT_HW, y=2)
-            tr = tr_tiles.pop(key)
+        def group_words(tr, grouped):
+            words = grouped.bitcast(F32).rearrange("p (j b y) -> p j b y", j=OUT_HW, y=2)
             for j in range(OUT_HW):
-                nc.scalar.copy(
-                    out=grouped_words[:, j, :, :], in_=tr[:, j : j + 2, :].rearrange("p y b -> p b y")
-                )
-            grouped_tiles[key] = grouped
+                nc.scalar.copy(out=words[:, j, :, :], in_=tr[:, j : j + 2, :].rearrange("p y b -> p b y"))
 
-        def quantise_patches(q):
-            codes = mx_pool.tile([P, OUT_HW, HALF], U32, align_bytes=64)
-            scales = mx_pool.tile([P, OUT_HW, HALF], U8, align_bytes=64)
-            grouped = grouped_tiles.pop(q)
+        def group_duo(r):
+            grouped = grouped_pool.tile([P, DUO, HALF * WIN], BF16, align_bytes=64)
+            for d in range(DUO):
+                group_words(tr_tiles.pop(r * DUO + d), grouped[:, d, :])
+            grouped_tiles[r] = grouped
+
+        def group_low(n):
+            grouped = low_pool.tile([P, HALF * WIN], BF16, align_bytes=64)
+            group_words(low_tr.pop(n), grouped[:])
+            low_grouped[n] = grouped
+
+        def quantise_duo(r):
+            codes = mx_pool.tile([P, OUT_HW, DUO, HALF], U32, align_bytes=64)
+            scales = mx_pool.tile([P, OUT_HW, DUO, HALF], U8, align_bytes=64)
+            grouped = grouped_tiles.pop(r)
             for i in range(OUT_HW):
                 nc.vector.quantize_mx(
-                    out=codes[:, i, :].bitcast(FP8X4), scales=scales[:, i, :], in_=grouped[:]
+                    out=codes[:, i, :, :].rearrange("p d c -> p (d c)").bitcast(FP8X4),
+                    scales=scales[:, i, :, :].rearrange("p d c -> p (d c)"),
+                    in_=grouped[:].rearrange("p d e -> p (d e)"),
                 )
-            mx_tiles[q] = (codes, scales)
+            mx_tiles[r] = (codes, scales)
 
         def quantise_low(n):
-            codes = r_pool.tile([P, HALF], U32, align_bytes=64)
-            scales = r_pool.tile([P, HALF], U8, align_bytes=64)
-            nc.vector.quantize_mx(
-                out=codes[:].bitcast(FP8X4), scales=scales[:], in_=grouped_tiles.pop(("low", n))[:]
-            )
-            mx_tiles[("low", n)] = (codes, scales)
+            codes = low_pool.tile([P, HALF], U32, align_bytes=64)
+            scales = low_pool.tile([P, HALF], U8, align_bytes=64)
+            nc.vector.quantize_mx(out=codes[:].bitcast(FP8X4), scales=scales[:], in_=low_grouped.pop(n)[:])
+            low_mx[n] = (codes, scales)
 
         def multiply(q):
             n, t = divmod(q, T)
-            codes, scales = mx_tiles.pop(q)
-            low_codes, low_scales = mx_tiles[("low", n)]
+            codes, scales = mx_tiles[q // DUO]
+            low_codes, low_scales = low_mx[n]
             acc = acc_pool.tile([P, POSITIONS, C_OUT], F32)
-            for j in range(OUT_HW):
-                half = slice(j * P, (j + 1) * P)
+
+            def one_pass(i, j, data, data_scales, w, w_s, start, stop):
                 nc.tensor.matmul_mx(
-                    out=acc[:, j, :],
-                    lhsT=codes[:, 0, half].bitcast(FP8X4),
-                    lhsT_scale=scales[:, 0, half],
-                    rhs=w_codes[:, 0, half].bitcast(FP8X4),
-                    rhs_scale=w_scales[:, 0, half],
-                    start=True,
-                    stop=True,
+                    out=acc[:, i * OUT_HW + j, :],
+                    lhsT=data.bitcast(FP8X4),
+                    lhsT_scale=data_scales,
+                    rhs=w.bitcast(FP8X4),
+                    rhs_scale=w_s,
+                    start=start,
+                    stop=stop,
                 )
-            for j in range(OUT_HW):
-                half = slice(j * P, (j + 1) * P)
-                nc.tensor.matmul_mx(
-                    out=acc[:, OUT_HW + j, :],
-                    lhsT=codes[:, 1, half].bitcast(FP8X4),
-                    lhsT_scale=scales[:, 1, half],
-                    rhs=w_codes[:, 1, half].bitcast(FP8X4),
-                    rhs_scale=w_scales[:, 1, half],
-                    start=True,
-                    stop=False,
-                )
-                nc.tensor.matmul_mx(
-                    out=acc[:, OUT_HW + j, :],
-                    lhsT=low_codes[:, half].bitcast(FP8X4),
-                    lhsT_scale=low_scales[:, half],
-                    rhs=w_low_codes[:, t, half].bitcast(FP8X4),
-                    rhs_scale=w_scales[:, 2, half],
-                    start=False,
-                    stop=True,
-                )
+
+            for i in range(OUT_HW):
+                for j in range(OUT_HW):
+                    half = slice(j * P, (j + 1) * P)
+                    part = (TOP, MID)[i]
+                    one_pass(
+                        i, j, codes[:, i, q % DUO, half], scales[:, i, q % DUO, half],
+                        w_codes[:, part, half], w_scales[:, part, half], True, i == 0,
+                    )
+                    if i == 1:
+                        one_pass(
+                            i, j, low_codes[:, half], low_scales[:, half],
+                            w_low_codes[:, t, half], w_scales[:, LOW, half], False, True,
+                        )
             acc_tiles[q] = acc
 
-        def store(q):
+        def store(q, copy):
             n, t = divmod(q, T)
             o_sb = o_pool.tile([P, C_OUT * POSITIONS], F32)
-            nc.scalar.copy(
+            copy(
                 out=o_sb[:].rearrange("p (k s) -> p k s", s=POSITIONS),
                 in_=acc_tiles.pop(q)[:].rearrange("p s k -> p k s"),
             )
             nc.sync.dma_start(out=out_view[n, :, t, :], in_=o_sb[:])
 
-        for step in range(TILES + 4):
-            group, t = divmod(step, T)
-            if step < TILES:
-                make_pairs(step)
-                transpose_pairs(step)
-                if step == 2 or (group > 0 and t == 0):
-                    make_low_pairs(group)
-                    transpose_pairs(("low", group))
-            if step == 0:
-                place_weights(TOP)
+        low_with = {max(n * T // DUO, 1): n for n in range(GROUPS)}
+        for step in range(DUOS + 4):
+            if step < DUOS:
+                for d in range(DUO):
+                    make_pairs(step * DUO + d)
+                if step in low_with:
+                    make_low_pairs(low_with[step])
+            if 0 <= step - 3 < DUOS:
+                for d in range(DUO):
+                    multiply((step - 3) * DUO + d)
+            if step < DUOS:
+                for d in range(DUO):
+                    tr_tiles[step * DUO + d] = transpose_words(z_tiles.pop(step * DUO + d))
+                if step in low_with:
+                    low_tr[low_with[step]] = transpose_words(low_z.pop(low_with[step]))
+            if 0 <= step - 1 < DUOS:
+                group_duo(step - 1)
             if step == 1:
-                place_weights(MID)
-            if 0 <= step - 1 < TILES:
-                group_words(step - 1)
-                if step == 3 or (0 < group < GROUPS and t == 1):
-                    group_words(("low", group))
-            if step == 2:
-                place_weights(LOW)
-                quantise_weights(TOP)
-                quantise_weights(MID)
-            if 0 <= step - 2 < TILES:
-                quantise_patches(step - 2)
-                if step == 3:
+                place_weights(TOP, nc.scalar.copy)
+                place_weights(MID, nc.vector.tensor_copy)
+                group_low(0)
+                place_weights(LOW, nc.scalar.copy)
+            elif step - 1 in low_with and step > 2:
+                group_low(low_with[step - 1])
+            if 0 <= step - 2 < DUOS:
+                if step == 2:
+                    quantise_weights(TOP)
+                    quantise_weights(MID)
+                quantise_duo(step - 2)
+                if step == 2:
+                    quantise_low(0)
                     quantise_weights(LOW)
                     spread_low_weights()
-                if step == 3 or (0 < group < GROUPS and t == 2):
-                    quantise_low(group)
-            if 0 <= step - 3 < TILES:
-                multiply(step - 3)
+                elif step - 2 in low_with and step > 3:
+                    quantise_low(low_with[step - 2])
             if 0 <= step - 4:
-                store(step - 4)
+                for d in range(DUO):
+                    last = step - 4 >= DUOS - 2
+                    store((step - 4) * DUO + d, nc.vector.tensor_copy if last and d == 1 else nc.scalar.copy)

@@ -70,15 +70,14 @@ def tile_stdpconvinhibit_t_kernel(tc, in_spikes, weights, out):
         make_identity(nc, identity[:])
 
         place = keep.tile([P, 3, WIN, C_IN], BF16)
-        nc.gpsimd.memset(place[:, MID, 0, :], 0.0)
+        nc.vector.memset(place[:, MID, 0, :], 0.0)
         by_row = identity[:].rearrange("p (g m u) -> p u m g", g=C_HI, m=C_LO, u=WIN)
-        for part, group, u in (
-            [(TOP, u, u) for u in range(WIN)]
-            + [(MID, u + 1, u) for u in range(WIN - 1)]
-            + [(LOW, group, WIN - 1) for group in range(T)]
+        for part, groups, rows in (
+            [(TOP, slice(0, WIN), slice(0, WIN)), (MID, slice(1, WIN), slice(0, WIN - 1))]
+            + [(LOW, slice(group, group + 1), slice(WIN - 1, WIN)) for group in range(T)]
         ):
-            nc.gpsimd.tensor_copy(
-                out=place[:, part, group, :].rearrange("p (m g) -> p m g", m=C_LO), in_=by_row[:, u, :, :]
+            nc.vector.tensor_copy(
+                out=place[:, part, groups, :].rearrange("p u (m g) -> p u m g", m=C_LO), in_=by_row[:, rows, :, :]
             )
 
         w_codes = keep.tile([P, 3, HALF], U32, align_bytes=64)
@@ -257,18 +256,17 @@ def tile_stdpconvinhibit_t_kernel(tc, in_spikes, weights, out):
                 group_duo(step - 1)
             if step == 1:
                 place_weights(TOP, nc.scalar.copy)
-                place_weights(MID, nc.vector.tensor_copy)
                 group_low(0)
-                place_weights(LOW, nc.scalar.copy)
+                place_weights(MID, nc.scalar.copy)
             elif step - 1 in low_with and step > 2:
                 group_low(low_with[step - 1])
             if 0 <= step - 2 < DUOS:
-                if step == 2:
-                    quantise_weights(TOP)
-                    quantise_weights(MID)
                 quantise_duo(step - 2)
                 if step == 2:
+                    place_weights(LOW, nc.vector.tensor_copy)
+                    quantise_weights(TOP)
                     quantise_low(0)
+                    quantise_weights(MID)
                     quantise_weights(LOW)
                     spread_low_weights()
                 elif step - 2 in low_with and step > 3:

@@ -82,11 +82,15 @@ def tile_stdpconvinhibit_t_kernel(tc, in_spikes, weights, out):
 
         w_codes = keep.tile([P, 3, HALF], U32, align_bytes=64)
         w_scales = keep.tile([P, 3, HALF], U8, align_bytes=64)
+        w_flat = w_codes[:].rearrange("p a c -> p (a c)")
+        w_scales_flat = w_scales[:].rearrange("p a c -> p (a c)")
         w_low_codes = keep.tile([P, T, HALF], U32, align_bytes=64)
         nc.gpsimd.memset(w_low_codes[:].bitcast(I32), 0)
         w_grouped = keep.tile([P, 3, HALF * WIN], BF16, align_bytes=64)
 
-        def place_weights(part, copy):
+        w_placed = {}
+
+        def place_weights(part):
             acc = acc_pool.tile([P, OUT_HW, C_OUT * WIN], BF16)
             for j, columns, words in (
                 (0, slice(0, 4, 1), slice(0, 4)),
@@ -102,7 +106,10 @@ def tile_stdpconvinhibit_t_kernel(tc, in_spikes, weights, out):
                     start=True,
                     stop=True,
                 )
-            copy(out=w_grouped[:, part, :], in_=acc[:].rearrange("p j e -> p (j e)"))
+            w_placed[part] = acc
+
+        def group_weights(part, copy):
+            copy(out=w_grouped[:, part, :], in_=w_placed.pop(part)[:].rearrange("p j e -> p (j e)"))
 
         def quantise_weights(part):
             nc.vector.quantize_mx(
@@ -202,9 +209,11 @@ def tile_stdpconvinhibit_t_kernel(tc, in_spikes, weights, out):
             low_codes, low_scales = low_mx[n]
             acc = acc_pool.tile([P, POSITIONS, C_OUT], F32)
 
-            def one_pass(i, j, data, data_scales, w, w_s, start, stop):
+            acc_flat = acc[:].rearrange("p s k -> p (s k)")
+
+            def one_pass(columns, data, data_scales, w, w_s, start, stop):
                 nc.tensor.matmul_mx(
-                    out=acc[:, i * OUT_HW + j, :],
+                    out=acc_flat[:, columns],
                     lhsT=data.bitcast(FP8X4),
                     lhsT_scale=data_scales,
                     rhs=w.bitcast(FP8X4),
@@ -213,19 +222,24 @@ def tile_stdpconvinhibit_t_kernel(tc, in_spikes, weights, out):
                     stop=stop,
                 )
 
-            for i in range(OUT_HW):
-                for j in range(OUT_HW):
-                    half = slice(j * P, (j + 1) * P)
-                    part = (TOP, MID)[i]
-                    one_pass(
-                        i, j, codes[:, i, q % DUO, half], scales[:, i, q % DUO, half],
-                        w_codes[:, part, half], w_scales[:, part, half], True, i == 0,
-                    )
-                    if i == 1:
-                        one_pass(
-                            i, j, low_codes[:, half], low_scales[:, half],
-                            w_low_codes[:, t, half], w_scales[:, LOW, half], False, True,
-                        )
+            for j in range(OUT_HW):
+                half = slice(j * P, (j + 1) * P)
+                wide = slice(j * P, (j + 2) * P)
+                one_pass(
+                    wide, codes[:, 0, q % DUO, half], scales[:, 0, q % DUO, half],
+                    w_flat[:, wide], w_scales_flat[:, wide], True, True,
+                )
+            for j in range(OUT_HW):
+                half = slice(j * P, (j + 1) * P)
+                place_of = slice((OUT_HW + j) * P, (OUT_HW + j + 1) * P)
+                one_pass(
+                    place_of, codes[:, 1, q % DUO, half], scales[:, 1, q % DUO, half],
+                    w_codes[:, MID, half], w_scales[:, MID, half], True, False,
+                )
+                one_pass(
+                    place_of, low_codes[:, half], low_scales[:, half],
+                    w_low_codes[:, t, half], w_scales[:, LOW, half], False, True,
+                )
             acc_tiles[q] = acc
 
         def store(q, copy):
@@ -239,6 +253,9 @@ def tile_stdpconvinhibit_t_kernel(tc, in_spikes, weights, out):
 
         low_with = {max(n * T // DUO, 1): n for n in range(GROUPS)}
         for step in range(DUOS + 4):
+            if step == 2:
+                quantise_duo(0)
+                group_weights(LOW, nc.vector.tensor_copy)
             if step < DUOS:
                 for d in range(DUO):
                     make_pairs(step * DUO + d)
@@ -250,26 +267,29 @@ def tile_stdpconvinhibit_t_kernel(tc, in_spikes, weights, out):
             if step < DUOS:
                 for d in range(DUO):
                     tr_tiles[step * DUO + d] = transpose_words(z_tiles.pop(step * DUO + d))
+                if step == 0:
+                    place_weights(TOP)
+                if step == 1:
+                    place_weights(MID)
+                    place_weights(LOW)
                 if step in low_with:
                     low_tr[low_with[step]] = transpose_words(low_z.pop(low_with[step]))
             if 0 <= step - 1 < DUOS:
                 group_duo(step - 1)
             if step == 1:
-                place_weights(TOP, nc.scalar.copy)
+                group_weights(TOP, nc.scalar.copy)
                 group_low(0)
-                place_weights(MID, nc.scalar.copy)
+                group_weights(MID, nc.scalar.copy)
             elif step - 1 in low_with and step > 2:
                 group_low(low_with[step - 1])
-            if 0 <= step - 2 < DUOS:
+            if step == 2:
+                for part in (TOP, MID, LOW):
+                    quantise_weights(part)
+                spread_low_weights()
+                quantise_low(0)
+            elif 0 <= step - 2 < DUOS:
                 quantise_duo(step - 2)
-                if step == 2:
-                    place_weights(LOW, nc.vector.tensor_copy)
-                    quantise_weights(TOP)
-                    quantise_low(0)
-                    quantise_weights(MID)
-                    quantise_weights(LOW)
-                    spread_low_weights()
-                elif step - 2 in low_with and step > 3:
+                if step - 2 in low_with and step > 3:
                     quantise_low(low_with[step - 2])
             if 0 <= step - 4:
                 for d in range(DUO):

@@ -29,6 +29,7 @@ TILES = BATCH // P
 DUO = 2
 DUOS = TILES // DUO
 HALF = OUT_HW * P
+GROUP_LAG, QUANTISE_LAG, MULTIPLY_LAG, OUT_LAG = 1, 3, 4, 5
 TOP, MID, LOW = range(3)
 
 FLOPS = 2 * BATCH * POSITIONS * C_IN * WIN * WIN * C_OUT
@@ -42,8 +43,8 @@ def tile_stdpconvinhibit_t_kernel(tc, in_spikes, weights, out):
     with ExitStack() as stack:
         keep = stack.enter_context(tc.tile_pool(name="keep", bufs=1))
         x_pool = stack.enter_context(tc.tile_pool(name="x", bufs=GROUPS))
-        z_pool = stack.enter_context(tc.tile_pool(name="z", bufs=6))
-        grouped_pool = stack.enter_context(tc.tile_pool(name="grouped", bufs=3))
+        z_pool = stack.enter_context(tc.tile_pool(name="z", bufs=8))
+        grouped_pool = stack.enter_context(tc.tile_pool(name="grouped", bufs=4))
         low_pool = stack.enter_context(tc.tile_pool(name="low", bufs=3))
         mx_pool = stack.enter_context(tc.tile_pool(name="mx", bufs=3))
         o_pool = stack.enter_context(tc.tile_pool(name="o", bufs=12))
@@ -60,8 +61,8 @@ def tile_stdpconvinhibit_t_kernel(tc, in_spikes, weights, out):
             if n == 0:
                 nc.sync.dma_start(out=x_sb[:, 0:1, :], in_=x_view[n, :, 0:1, :])
                 nc.sync.dma_start(out=x_sb[:, 1:2, :], in_=x_view[n, :, 1:2, :])
-                nc.sync.dma_start(out=w_raw[:, 0:OUT_HW, :], in_=w_view[:, 0:OUT_HW, :])
                 nc.sync.dma_start(out=x_sb[:, 2:4, :], in_=x_view[n, :, 2:4, :])
+                nc.sync.dma_start(out=w_raw[:, 0:OUT_HW, :], in_=w_view[:, 0:OUT_HW, :])
                 nc.sync.dma_start(out=w_raw[:, OUT_HW:POSITIONS, :], in_=w_view[:, OUT_HW:POSITIONS, :])
             else:
                 nc.sync.dma_start(out=x_sb[:], in_=x_view[n])
@@ -252,7 +253,7 @@ def tile_stdpconvinhibit_t_kernel(tc, in_spikes, weights, out):
             nc.sync.dma_start(out=out_view[n, :, t, :], in_=o_sb[:])
 
         low_with = {max(n * T // DUO, 1): n for n in range(GROUPS)}
-        for step in range(DUOS + 4):
+        for step in range(DUOS + OUT_LAG):
             if step == 2:
                 quantise_duo(0)
                 group_weights(LOW, nc.vector.tensor_copy)
@@ -261,9 +262,9 @@ def tile_stdpconvinhibit_t_kernel(tc, in_spikes, weights, out):
                     make_pairs(step * DUO + d)
                 if step in low_with:
                     make_low_pairs(low_with[step])
-            if 0 <= step - 3 < DUOS:
+            if 0 <= step - MULTIPLY_LAG < DUOS:
                 for d in range(DUO):
-                    multiply((step - 3) * DUO + d)
+                    multiply((step - MULTIPLY_LAG) * DUO + d)
             if step < DUOS:
                 for d in range(DUO):
                     tr_tiles[step * DUO + d] = transpose_words(z_tiles.pop(step * DUO + d))
@@ -274,24 +275,24 @@ def tile_stdpconvinhibit_t_kernel(tc, in_spikes, weights, out):
                     place_weights(LOW)
                 if step in low_with:
                     low_tr[low_with[step]] = transpose_words(low_z.pop(low_with[step]))
-            if 0 <= step - 1 < DUOS:
-                group_duo(step - 1)
-            if step == 1:
-                group_weights(TOP, nc.scalar.copy)
-                group_low(0)
-                group_weights(MID, nc.scalar.copy)
-            elif step - 1 in low_with and step > 2:
-                group_low(low_with[step - 1])
-            if step == 2:
+            if 0 <= step - OUT_LAG:
+                for d in range(DUO):
+                    last = step - OUT_LAG >= DUOS - 2
+                    store((step - OUT_LAG) * DUO + d, nc.vector.tensor_copy if last and d == 1 else nc.scalar.copy)
+            if 0 <= step - GROUP_LAG < DUOS:
+                group_duo(step - GROUP_LAG)
+                if step == 1:
+                    group_weights(TOP, nc.scalar.copy)
+                if step - GROUP_LAG in low_with:
+                    group_low(low_with[step - GROUP_LAG])
+                if step == 2:
+                    group_weights(MID, nc.scalar.copy)
+            if step == QUANTISE_LAG:
                 for part in (TOP, MID, LOW):
                     quantise_weights(part)
                 spread_low_weights()
                 quantise_low(0)
-            elif 0 <= step - 2 < DUOS:
-                quantise_duo(step - 2)
-                if step - 2 in low_with and step > 3:
-                    quantise_low(low_with[step - 2])
-            if 0 <= step - 4:
-                for d in range(DUO):
-                    last = step - 4 >= DUOS - 2
-                    store((step - 4) * DUO + d, nc.vector.tensor_copy if last and d == 1 else nc.scalar.copy)
+            elif 0 <= step - QUANTISE_LAG < DUOS:
+                quantise_duo(step - QUANTISE_LAG)
+                if step - QUANTISE_LAG in low_with and step - QUANTISE_LAG > 1:
+                    quantise_low(low_with[step - QUANTISE_LAG])

@@ -144,11 +144,14 @@ def tile_stdpconvinhibit_t_kernel(tc, in_spikes, weights, out):
             image = x_tiles[q // T][:, q % T, :].rearrange(
                 "p (g m h w) -> p m h g w", g=C_HI, m=C_LO, h=IMG, w=IMG
             )[:, :, 0:WIN, :, :]
-            for z, width, columns in ((quads, 4, slice(0, 4, 1)), (pairs, 2, slice(1, 5, 3))):
-                nc.vector.tensor_copy(
-                    out=z[:].rearrange("p (h m g e) -> p m h g e", h=WIN, m=C_LO, g=C_HI, e=width),
-                    in_=image[:, :, :, :, columns],
-                )
+            for z, width, columns, span in ((quads, 4, slice(0, 4, 1), C_HI // 2), (pairs, 2, slice(1, 5, 3), C_HI)):
+                for g in range(0, C_HI, span):
+                    nc.vector.tensor_copy(
+                        out=z[:].rearrange("p (h m g e) -> p m h g e", h=WIN, m=C_LO, g=C_HI, e=width)[
+                            :, :, :, g : g + span, :
+                        ],
+                        in_=image[:, :, :, g : g + span, columns],
+                    )
             z_tiles[q] = (quads, pairs)
 
         def make_low_pairs(n):

from contextlib import ExitStack

import concourse.mybir as mybir
from concourse.masks import make_identity

BF16 = mybir.dt.bfloat16
F32 = mybir.dt.float32
I32 = mybir.dt.int32
U32 = mybir.dt.uint32
U8 = mybir.dt.uint8
FP8X4 = mybir.dt.float8_e4m3fn_x4

P = 128
BATCH = 4096
C_IN = 32
C_OUT = 128
IMG = 5
WIN = 4
OUT_HW = 2
POSITIONS = OUT_HW * OUT_HW
PIXELS = C_IN * IMG * IMG
T = 4
GROUPS = BATCH // (P * T)

C_HI = 4
C_LO = 8

TILES = BATCH // P
DUO = 2
DUOS = TILES // DUO
HALF = OUT_HW * P
GROUP_LAG, QUANTISE_LAG, MULTIPLY_LAG, OUT_LAG = 1, 3, 4, 5
TOP, MID, LOW = range(3)

FLOPS = 2 * BATCH * POSITIONS * C_IN * WIN * WIN * C_OUT


def tile_stdpconvinhibit_t_kernel(tc, in_spikes, weights, out):
    nc = tc.nc
    x_view = in_spikes.rearrange("(n p t) c h w -> n p t (c h w)", p=P, t=T)
    out_view = out.rearrange("(n p t) k i j -> n p t (k i j)", p=P, t=T)

    with ExitStack() as stack:
        keep = stack.enter_context(tc.tile_pool(name="keep", bufs=1))
        x_pool = stack.enter_context(tc.tile_pool(name="x", bufs=GROUPS))
        z_pool = stack.enter_context(tc.tile_pool(name="z", bufs=8))
        grouped_pool = stack.enter_context(tc.tile_pool(name="grouped", bufs=4))
        low_pool = stack.enter_context(tc.tile_pool(name="low", bufs=3))
        mx_pool = stack.enter_context(tc.tile_pool(name="mx", bufs=3))
        o_pool = stack.enter_context(tc.tile_pool(name="o", bufs=12))
        tr_pool = stack.enter_context(tc.psum_pool(name="tr", bufs=4))
        acc_pool = stack.enter_context(tc.psum_pool(name="acc", bufs=4))
        stack.enter_context(tc.manual_schedule())

        w_raw = keep.tile([P, POSITIONS, WIN * C_OUT], BF16)
        w_view = weights.rearrange("i j c u v k -> (c u) (i j) (v k)")
        x_tiles = []
        for n in range(GROUPS):
            x_sb = x_pool.tile([P, T, PIXELS], BF16)
            x_tiles.append(x_sb)
            if n == 0:
                nc.sync.dma_start(out=x_sb[:, 0:1, :], in_=x_view[n, :, 0:1, :])
                nc.sync.dma_start(out=x_sb[:, 1:2, :], in_=x_view[n, :, 1:2, :])
                nc.sync.dma_start(out=x_sb[:, 2:4, :], in_=x_view[n, :, 2:4, :])
                nc.sync.dma_start(out=w_raw[:, 0:OUT_HW, :], in_=w_view[:, 0:OUT_HW, :])
                nc.sync.dma_start(out=w_raw[:, OUT_HW:POSITIONS, :], in_=w_view[:, OUT_HW:POSITIONS, :])
            else:
                nc.sync.dma_start(out=x_sb[:], in_=x_view[n])

        identity = keep.tile([P, P], F32)
        make_identity(nc, identity[:])

        place = keep.tile([P, 3, WIN, C_IN], BF16)
        nc.vector.memset(place[:, MID, 0, :], 0.0)
        by_row = identity[:].rearrange("p (g m u) -> p u m g", g=C_HI, m=C_LO, u=WIN)
        for part, groups, rows in (
            [(TOP, slice(0, WIN), slice(0, WIN)), (MID, slice(1, WIN), slice(0, WIN - 1))]
            + [(LOW, slice(group, group + 1), slice(WIN - 1, WIN)) for group in range(T)]
        ):
            nc.vector.tensor_copy(
                out=place[:, part, groups, :].rearrange("p u (m g) -> p u m g", m=C_LO), in_=by_row[:, rows, :, :]
            )

        w_codes = keep.tile([P, 3, HALF], U32, align_bytes=64)
        w_scales = keep.tile([P, 3, HALF], U8, align_bytes=64)
        w_flat = w_codes[:].rearrange("p a c -> p (a c)")
        w_scales_flat = w_scales[:].rearrange("p a c -> p (a c)")
        w_low_codes = keep.tile([P, T, HALF], U32, align_bytes=64)
        nc.gpsimd.memset(w_low_codes[:].bitcast(I32), 0)
        w_grouped = keep.tile([P, 3, HALF * WIN], BF16, align_bytes=64)

        w_placed = {}

        def place_weights(part):
            acc = acc_pool.tile([P, OUT_HW, C_OUT * WIN], BF16)
            for j, columns, words in (
                (0, slice(0, 4, 1), slice(0, 4)),
                (1, slice(1, 3, 1), slice(0, 2)),
                (1, slice(0, 4, 3), slice(2, 4)),
            ):
                nc.tensor.matmul(
                    acc[:, j, :].rearrange("p (k t) -> p t k", t=WIN)[:, words, :],
                    lhsT=place[:, part, :, :].rearrange("p u c -> p (u c)"),
                    rhs=w_raw[:, (0 if part == TOP else OUT_HW) + j, :].rearrange("p (v k) -> p v k", v=WIN)[
                        :, columns, :
                    ],
                    start=True,
                    stop=True,
                )
            w_placed[part] = acc

        def group_weights(part, copy):
            copy(out=w_grouped[:, part, :], in_=w_placed.pop(part)[:].rearrange("p j e -> p (j e)"))

        def quantise_weights(part):
            nc.vector.quantize_mx(
                out=w_codes[:, part, :].bitcast(FP8X4), scales=w_scales[:, part, :], in_=w_grouped[:, part, :]
            )

        def spread_low_weights():
            for t in range(T):
                rows = slice(t * C_IN, (t + 1) * C_IN)
                nc.vector.tensor_copy(
                    out=w_low_codes[rows, t, :].bitcast(I32), in_=w_codes[rows, LOW, :].bitcast(I32)
                )

        z_tiles = {}
        low_z = {}
        tr_tiles = {}
        low_tr = {}
        grouped_tiles = {}
        low_grouped = {}
        mx_tiles = {}
        low_mx = {}
        acc_tiles = {}

        def new_z():
            quads = z_pool.tile([P, P * 4], BF16)
            pairs = z_pool.tile([P, P * 2], BF16)
            return quads, pairs

        def make_pairs(q):
            quads, pairs = new_z()
            image = x_tiles[q // T][:, q % T, :].rearrange(
                "p (g m h w) -> p m h g w", g=C_HI, m=C_LO, h=IMG, w=IMG
            )[:, :, 0:WIN, :, :]
            for z, width, columns, span in ((quads, 4, slice(0, 4, 1), C_HI // 2), (pairs, 2, slice(1, 5, 3), C_HI)):
                for g in range(0, C_HI, span):
                    nc.vector.tensor_copy(
                        out=z[:].rearrange("p (h m g e) -> p m h g e", h=WIN, m=C_LO, g=C_HI, e=width)[
                            :, :, :, g : g + span, :
                        ],
                        in_=image[:, :, :, g : g + span, columns],
                    )
            z_tiles[q] = (quads, pairs)

        def make_low_pairs(n):
            quads, pairs = new_z()
            image = x_tiles[n][:].rearrange(
                "p t (g m h w) -> p m t h g w", g=C_HI, m=C_LO, h=IMG, w=IMG
            )[:, :, :, IMG - 1, :, :]
            for z, width, columns in ((quads, 4, slice(0, 4, 1)), (pairs, 2, slice(1, 5, 3))):
                nc.vector.tensor_copy(
                    out=z[:].rearrange("p (t m g e) -> p m t g e", t=T, m=C_LO, g=C_HI, e=width),
                    in_=image[:, :, :, :, columns],
                )
            low_z[n] = (quads, pairs)

        def transpose_words(z):
            quads, pairs = (part[:].bitcast(F32) for part in z)
            tr = tr_pool.tile([P, 3, P], F32)
            for plane, words in enumerate((quads[:, 0 : 2 * P : 2], quads[:, 1 : 2 * P : 2], pairs)):
                nc.tensor.transpose(tr[:, plane, :], words, identity[:])
            return tr

        def group_words(tr, grouped):
            words = grouped.bitcast(F32).rearrange("p (j b y) -> p j b y", j=OUT_HW, y=2)
            for j in range(OUT_HW):
                nc.scalar.copy(out=words[:, j, :, :], in_=tr[:, j : j + 2, :].rearrange("p y b -> p b y"))

        def group_duo(r):
            grouped = grouped_pool.tile([P, DUO, HALF * WIN], BF16, align_bytes=64)
            for d in range(DUO):
                group_words(tr_tiles.pop(r * DUO + d), grouped[:, d, :])
            grouped_tiles[r] = grouped

        def group_low(n):
            grouped = low_pool.tile([P, HALF * WIN], BF16, align_bytes=64)
            group_words(low_tr.pop(n), grouped[:])
            low_grouped[n] = grouped

        def quantise_duo(r):
            codes = mx_pool.tile([P, OUT_HW, DUO, HALF], U32, align_bytes=64)
            scales = mx_pool.tile([P, OUT_HW, DUO, HALF], U8, align_bytes=64)
            grouped = grouped_tiles.pop(r)
            for i in range(OUT_HW):
                nc.vector.quantize_mx(
                    out=codes[:, i, :, :].rearrange("p d c -> p (d c)").bitcast(FP8X4),
                    scales=scales[:, i, :, :].rearrange("p d c -> p (d c)"),
                    in_=grouped[:].rearrange("p d e -> p (d e)"),
                )
            mx_tiles[r] = (codes, scales)

        def quantise_low(n):
            codes = low_pool.tile([P, HALF], U32, align_bytes=64)
            scales = low_pool.tile([P, HALF], U8, align_bytes=64)
            nc.vector.quantize_mx(out=codes[:].bitcast(FP8X4), scales=scales[:], in_=low_grouped.pop(n)[:])
            low_mx[n] = (codes, scales)

        def multiply(q):
            n, t = divmod(q, T)
            codes, scales = mx_tiles[q // DUO]
            low_codes, low_scales = low_mx[n]
            acc = acc_pool.tile([P, POSITIONS, C_OUT], F32)

            acc_flat = acc[:].rearrange("p s k -> p (s k)")

            def one_pass(columns, data, data_scales, w, w_s, start, stop):
                nc.tensor.matmul_mx(
                    out=acc_flat[:, columns],
                    lhsT=data.bitcast(FP8X4),
                    lhsT_scale=data_scales,
                    rhs=w.bitcast(FP8X4),
                    rhs_scale=w_s,
                    start=start,
                    stop=stop,
                )

            for j in range(OUT_HW):
                half = slice(j * P, (j + 1) * P)
                wide = slice(j * P, (j + 2) * P)
                one_pass(
                    wide, codes[:, 0, q % DUO, half], scales[:, 0, q % DUO, half],
                    w_flat[:, wide], w_scales_flat[:, wide], True, True,
                )
            for j in range(OUT_HW):
                half = slice(j * P, (j + 1) * P)
                place_of = slice((OUT_HW + j) * P, (OUT_HW + j + 1) * P)
                one_pass(
                    place_of, codes[:, 1, q % DUO, half], scales[:, 1, q % DUO, half],
                    w_codes[:, MID, half], w_scales[:, MID, half], True, False,
                )
                one_pass(
                    place_of, low_codes[:, half], low_scales[:, half],
                    w_low_codes[:, t, half], w_scales[:, LOW, half], False, True,
                )
            acc_tiles[q] = acc

        def store(q, copy):
            n, t = divmod(q, T)
            o_sb = o_pool.tile([P, C_OUT * POSITIONS], F32)
            copy(
                out=o_sb[:].rearrange("p (k s) -> p k s", s=POSITIONS),
                in_=acc_tiles.pop(q)[:].rearrange("p s k -> p k s"),
            )
            nc.sync.dma_start(out=out_view[n, :, t, :], in_=o_sb[:])

        low_with = {max(n * T // DUO, 1): n for n in range(GROUPS)}
        for step in range(DUOS + OUT_LAG):
            if step == 2:
                quantise_duo(0)
                group_weights(LOW, nc.vector.tensor_copy)
            if step < DUOS:
                for d in range(DUO):
                    make_pairs(step * DUO + d)
                if step in low_with:
                    make_low_pairs(low_with[step])
            if 0 <= step - MULTIPLY_LAG < DUOS:
                for d in range(DUO):
                    multiply((step - MULTIPLY_LAG) * DUO + d)
            if step < DUOS:
                for d in range(DUO):
                    tr_tiles[step * DUO + d] = transpose_words(z_tiles.pop(step * DUO + d))
                if step == 0:
                    place_weights(TOP)
                if step == 1:
                    place_weights(MID)
                    place_weights(LOW)
                if step in low_with:
                    low_tr[low_with[step]] = transpose_words(low_z.pop(low_with[step]))
            if 0 <= step - OUT_LAG:
                for d in range(DUO):
                    last = step - OUT_LAG >= DUOS - 2
                    store((step - OUT_LAG) * DUO + d, nc.vector.tensor_copy if last and d == 1 else nc.scalar.copy)
            if 0 <= step - GROUP_LAG < DUOS:
                group_duo(step - GROUP_LAG)
                if step == 1:
                    group_weights(TOP, nc.scalar.copy)
                if step - GROUP_LAG in low_with:
                    group_low(low_with[step - GROUP_LAG])
                if step == 2:
                    group_weights(MID, nc.scalar.copy)
            if step == QUANTISE_LAG:
                for part in (TOP, MID, LOW):
                    quantise_weights(part)
                spread_low_weights()
                quantise_low(0)
            elif 0 <= step - QUANTISE_LAG < DUOS:
                quantise_duo(step - QUANTISE_LAG)
                if step - QUANTISE_LAG in low_with and step - QUANTISE_LAG > 1:
                    quantise_low(low_with[step - QUANTISE_LAG])
